import numpy as np
import ml_dtypes

BF16 = ml_dtypes.bfloat16


def bf(x):
    return np.asarray(x, np.float32).astype(BF16)


def f32(x):
    return np.asarray(x, np.float32)


def f64(x):
    return np.asarray(x).astype(np.float64)


def striped(idx):
    return np.tile(idx.reshape(-1, 16).T, (8, 1))


C, S, N, U, K = 1024, 256, 128, 256, 8
BETA = 0.5
EPS = 1e-8
GAIN = 2.0


def setup_inputs():
    adj = np.random.random((U, U)) * (np.random.random((U, U)) < K / U) + np.eye(U)
    return {"base": f32(np.random.standard_normal((C, S))), "x": f32(np.random.standard_normal((C, U))), "w_gcn": f32(GAIN * np.random.standard_normal((C, C)) / np.sqrt(C)), "adj": f32(adj), "offs": striped(np.random.permutation(S)[:N])}


def reference(base, x, w_gcn, adj, offs):
    idx = offs[:16].T.reshape(-1)
    a = f64(adj)
    d = 1.0 / np.sqrt(a.sum(axis=1) + EPS)
    h = f64(x).T @ f64(w_gcn)
    ahat = d[:N, None] * a[:N] * d[None, :]
    z = (ahat @ h).T
    out = f64(base).copy()
    out[:, idx] = f64(x)[:, :N] + BETA * np.maximum(z, 0.0)
    return out

@@ -1,0 +1,111 @@
+import concourse.mybir as mybir
+from concourse.masks import make_identity
+
+P = 128
+C, S, N, U = 1024, 256, 128, 256
+EPS = 1e-8
+BETA = 0.5
+PAIRS = C // (2 * P)
+NODE_BLOCKS = U // P
+FLOPS = 2 * U * C * C + 2 * N * U * C
+
+F32 = mybir.dt.float32
+BF16 = mybir.dt.bfloat16
+U16 = mybir.dt.uint16
+ACT = mybir.ActivationFunctionType
+
+
+def tile_structureawaregcn_kernel(tc, base, x, w_gcn, adj, offs, out):
+    nc = tc.nc
+    base_pairs = base.rearrange("(r i p) s -> r p i s", i=2, p=P)
+    out_pairs = out.rearrange("(r i p) s -> r p i s", i=2, p=P)
+    x_pairs = x.rearrange("(r i p) u -> r p i u", i=2, p=P)
+    w_pairs = w_gcn.rearrange("(r i p) c -> r p i c", i=2, p=P)
+
+    with (
+        tc.tile_pool(name="held", bufs=1) as held,
+        tc.tile_pool(name="work", bufs=2) as work,
+        tc.psum_pool(name="psum_once", bufs=1) as psum_once,
+        tc.psum_pool(name="psum", bufs=2) as psum,
+    ):
+        offsets = held.tile([P, N // 16], U16, name="offsets")
+        nc.sync.dma_start(offsets[:], offs)
+        adj_rows = held.tile([P, NODE_BLOCKS, U], F32, name="adj_rows")
+        nc.sync.dma_start(adj_rows[:], adj.rearrange("(t p) v -> p t v", p=P))
+        x_raw = []
+        for r in range(PAIRS):
+            x_raw.append(held.tile([P, 2, U], F32, name=f"x_raw{r}"))
+            nc.sync.dma_start(x_raw[r][:], x_pairs[r])
+        windows = {}
+        w_raw = {}
+        for q in range(PAIRS):
+            for i in range(2):
+                windows[q, i] = held.tile([P, S], F32, name=f"window{q}_{i}")
+                nc.sync.dma_start(windows[q, i][:], base_pairs[q][:, i, :])
+            for r in range(PAIRS):
+                w_raw[q, r] = held.tile([P, 2, 2 * P], F32, name=f"w_raw{q}_{r}")
+                nc.sync.dma_start(w_raw[q, r][:], w_pairs[r][:, :, q * 2 * P : (q + 1) * 2 * P])
+
+        identity = held.tile([P, P], F32, name="identity")
+        make_identity(nc, identity[:])
+        deg = held.tile([P, NODE_BLOCKS], F32, name="deg")
+        nc.vector.reduce_sum(deg[:], adj_rows[:], axis=mybir.AxisListType.X)
+        root = held.tile([P, NODE_BLOCKS], F32, name="root")
+        nc.scalar.activation(root[:], deg[:], ACT.Sqrt, bias=EPS)
+        d = held.tile([P, NODE_BLOCKS], F32, name="d")
+        nc.vector.reciprocal(d[:], root[:])
+        scaled_rows = held.tile([P, U], F32, name="scaled_rows")
+        nc.vector.tensor_scalar_mul(scaled_rows[:], adj_rows[:, 0, :], d[:, 0:1])
+        flipped = psum_once.tile([P, NODE_BLOCKS, N], F32, name="flipped")
+        ahat_t = held.tile([P, NODE_BLOCKS, N], BF16, name="ahat_t")
+        for t in range(NODE_BLOCKS):
+            nc.tensor.transpose(flipped[:, t, :], scaled_rows[:, t * P : (t + 1) * P], identity[:])
+            nc.vector.tensor_scalar_mul(ahat_t[:, t, :], flipped[:, t, :], d[:, t : t + 1])
+
+        def cast_pair(name, raw):
+            first = held.tile([P, 2 * P], BF16, name=f"{name}_first")
+            second = held.tile([P, 2 * P], BF16, name=f"{name}_second")
+            nc.vector.tensor_copy(first[:], raw[:, 0, :])
+            nc.scalar.copy(second[:], raw[:, 1, :])
+            return first, second
+
+        x_bf = [cast_pair(f"x_bf{r}", x_raw[r]) for r in range(PAIRS)]
+
+        for q in range(PAIRS):
+            h_acc = [psum.tile([P, 2 * P], F32, name=f"h_acc{t}") for t in range(NODE_BLOCKS)]
+            for r in range(PAIRS):
+                w_bf = cast_pair(f"w_bf{q}_{r}", w_raw[q, r])
+                for i in range(2):
+                    for t in range(NODE_BLOCKS):
+                        nc.tensor.matmul(
+                            h_acc[t][:],
+                            x_bf[r][i][:, t * P : (t + 1) * P],
+                            w_bf[i][:],
+                            start=(r == 0 and i == 0),
+                            stop=(r == PAIRS - 1 and i == 1),
+                        )
+            h_bf = [work.tile([P, 2 * P], BF16, name=f"h_bf{t}") for t in range(NODE_BLOCKS)]
+            nc.vector.tensor_copy(h_bf[0][:], h_acc[0][:])
+            nc.scalar.copy(h_bf[1][:], h_acc[1][:])
+
+            z_acc = psum.tile([P, 2, N], F32, name="z_acc")
+            for i in range(2):
+                for t in range(NODE_BLOCKS):
+                    nc.tensor.matmul(
+                        z_acc[:, i, :],
+                        h_bf[t][:, i * P : (i + 1) * P],
+                        ahat_t[:, t, :],
+                        start=(t == 0),
+                        stop=(t == NODE_BLOCKS - 1),
+                    )
+            half_relu = work.tile([P, 2, N], F32, name="half_relu")
+            nc.scalar.activation(half_relu[:], z_acc[:], ACT.Relu, scale=BETA)
+
+            for i in range(2):
+                nc.vector.tensor_tensor(
+                    windows[q, i][:].indirect(offsets[:]),
+                    x_raw[q][:, i, 0:N],
+                    half_relu[:, i, :],
+                    mybir.AluOpType.add,
+                )
+                nc.sync.dma_start(out_pairs[q][:, i, :], windows[q, i][:])

@@ -5,8 +5,13 @@ P = 128
 C, S, N, U = 1024, 256, 128, 256
 EPS = 1e-8
 BETA = 0.5
-PAIRS = C // (2 * P)
+CHUNKS = 4
+CHUNK = C // CHUNKS
+CHUNK_BLOCKS = CHUNK // P
+LOADS = 2
+LOAD_BLOCKS = C // (P * LOADS)
 NODE_BLOCKS = U // P
+BLOCKS = C // P
 FLOPS = 2 * U * C * C + 2 * N * U * C
 
 F32 = mybir.dt.float32
@@ -17,37 +22,42 @@ ACT = mybir.ActivationFunctionType
 
 def tile_structureawaregcn_kernel(tc, base, x, w_gcn, adj, offs, out):
     nc = tc.nc
-    base_pairs = base.rearrange("(r i p) s -> r p i s", i=2, p=P)
-    out_pairs = out.rearrange("(r i p) s -> r p i s", i=2, p=P)
-    x_pairs = x.rearrange("(r i p) u -> r p i u", i=2, p=P)
-    w_pairs = w_gcn.rearrange("(r i p) c -> r p i c", i=2, p=P)
+    base_blocks = base.rearrange("(b p) s -> b p s", p=P)
+    out_blocks = out.rearrange("(b p) s -> b p s", p=P)
+    x_loads = x.rearrange("(g b p) u -> g p b u", b=LOAD_BLOCKS, p=P)
+    w_loads = w_gcn.rearrange("(g b p) c -> g p b c", b=LOAD_BLOCKS, p=P)
 
     with (
         tc.tile_pool(name="held", bufs=1) as held,
-        tc.tile_pool(name="work", bufs=2) as work,
+        tc.tile_pool(name="work", bufs=4) as work,
         tc.psum_pool(name="psum_once", bufs=1) as psum_once,
         tc.psum_pool(name="psum", bufs=2) as psum,
     ):
-        offsets = held.tile([P, N // 16], U16, name="offsets")
-        nc.sync.dma_start(offsets[:], offs)
-        adj_rows = held.tile([P, NODE_BLOCKS, U], F32, name="adj_rows")
-        nc.sync.dma_start(adj_rows[:], adj.rearrange("(t p) v -> p t v", p=P))
-        x_raw = []
-        for r in range(PAIRS):
-            x_raw.append(held.tile([P, 2, U], F32, name=f"x_raw{r}"))
-            nc.sync.dma_start(x_raw[r][:], x_pairs[r])
-        windows = {}
-        w_raw = {}
-        for q in range(PAIRS):
-            for i in range(2):
-                windows[q, i] = held.tile([P, S], F32, name=f"window{q}_{i}")
-                nc.sync.dma_start(windows[q, i][:], base_pairs[q][:, i, :])
-            for r in range(PAIRS):
-                w_raw[q, r] = held.tile([P, 2, 2 * P], F32, name=f"w_raw{q}_{r}")
-                nc.sync.dma_start(w_raw[q, r][:], w_pairs[r][:, :, q * 2 * P : (q + 1) * 2 * P])
-
         identity = held.tile([P, P], F32, name="identity")
         make_identity(nc, identity[:])
+
+        x_raw = [held.tile([P, LOAD_BLOCKS, U], F32, name=f"x_raw{g}") for g in range(LOADS)]
+        w_raw = [
+            [held.tile([P, LOAD_BLOCKS, CHUNK], F32, name=f"w_raw{q}_{g}") for g in range(LOADS)]
+            for q in range(CHUNKS)
+        ]
+        windows = [held.tile([P, S], F32, name=f"window{b}") for b in range(BLOCKS)]
+        offsets = held.tile([P, N // 16], U16, name="offsets")
+        adj_rows = held.tile([P, NODE_BLOCKS, U], F32, name="adj_rows")
+
+        nc.gpsimd.dma_start(adj_rows[:], adj.rearrange("(t p) v -> p t v", p=P))
+        for b in range(BLOCKS // 2):
+            nc.gpsimd.dma_start(windows[b][:], base_blocks[b])
+        for q in range(CHUNKS):
+            for g in range(LOADS):
+                if q == 0:
+                    nc.sync.dma_start(x_raw[g][:], x_loads[g])
+                nc.sync.dma_start(w_raw[q][g][:], w_loads[g][:, :, q * CHUNK : (q + 1) * CHUNK])
+            if q == 0:
+                nc.sync.dma_start(offsets[:], offs)
+        for b in range(BLOCKS // 2, BLOCKS):
+            nc.sync.dma_start(windows[b][:], base_blocks[b])
+
         deg = held.tile([P, NODE_BLOCKS], F32, name="deg")
         nc.vector.reduce_sum(deg[:], adj_rows[:], axis=mybir.AxisListType.X)
         root = held.tile([P, NODE_BLOCKS], F32, name="root")
@@ -62,50 +72,48 @@ def tile_structureawaregcn_kernel(tc, base, x, w_gcn, adj, offs, out):
             nc.tensor.transpose(flipped[:, t, :], scaled_rows[:, t * P : (t + 1) * P], identity[:])
             nc.vector.tensor_scalar_mul(ahat_t[:, t, :], flipped[:, t, :], d[:, t : t + 1])
 
-        def cast_pair(name, raw):
-            first = held.tile([P, 2 * P], BF16, name=f"{name}_first")
-            second = held.tile([P, 2 * P], BF16, name=f"{name}_second")
-            nc.vector.tensor_copy(first[:], raw[:, 0, :])
-            nc.scalar.copy(second[:], raw[:, 1, :])
-            return first, second
+        def cast_load(name, raw):
+            half = LOAD_BLOCKS // 2
+            width = raw.shape[2]
+            by_vector = held.tile([P, half, width], BF16, name=f"{name}_v")
+            by_scalar = held.tile([P, half, width], BF16, name=f"{name}_s")
+            nc.vector.tensor_copy(by_vector[:], raw[:, 0:half, :])
+            nc.scalar.copy(by_scalar[:], raw[:, half:LOAD_BLOCKS, :])
+            return [by_vector[:, b, :] for b in range(half)] + [by_scalar[:, b, :] for b in range(half)]
 
-        x_bf = [cast_pair(f"x_bf{r}", x_raw[r]) for r in range(PAIRS)]
+        x_bf = [cast_load(f"x_bf{g}", x_raw[g]) for g in range(LOADS)]
 
-        for q in range(PAIRS):
-            h_acc = [psum.tile([P, 2 * P], F32, name=f"h_acc{t}") for t in range(NODE_BLOCKS)]
-            for r in range(PAIRS):
-                w_bf = cast_pair(f"w_bf{q}_{r}", w_raw[q, r])
-                for i in range(2):
+        for q in range(CHUNKS):
+            h_acc = [psum.tile([P, CHUNK], F32, name=f"h_acc{t}") for t in range(NODE_BLOCKS)]
+            for g in range(LOADS):
+                w_bf = cast_load(f"w_bf{q}_{g}", w_raw[q][g])
+                for b in range(LOAD_BLOCKS):
                     for t in range(NODE_BLOCKS):
                         nc.tensor.matmul(
                             h_acc[t][:],
-                            x_bf[r][i][:, t * P : (t + 1) * P],
-                            w_bf[i][:],
-                            start=(r == 0 and i == 0),
-                            stop=(r == PAIRS - 1 and i == 1),
+                            x_bf[g][b][:, t * P : (t + 1) * P],
+                            w_bf[b],
+                            start=(g == 0 and b == 0),
+                            stop=(g == LOADS - 1 and b == LOAD_BLOCKS - 1),
                         )
-            h_bf = [work.tile([P, 2 * P], BF16, name=f"h_bf{t}") for t in range(NODE_BLOCKS)]
-            nc.vector.tensor_copy(h_bf[0][:], h_acc[0][:])
-            nc.scalar.copy(h_bf[1][:], h_acc[1][:])
+            for i in range(CHUNK_BLOCKS):
+                b = q * CHUNK_BLOCKS + i
+                h_bf = [work.tile([P, P], BF16, name=f"h_bf{t}") for t in range(NODE_BLOCKS)]
+                nc.vector.tensor_copy(h_bf[0][:], h_acc[0][:, i * P : (i + 1) * P])
+                nc.scalar.copy(h_bf[1][:], h_acc[1][:, i * P : (i + 1) * P])
 
-            z_acc = psum.tile([P, 2, N], F32, name="z_acc")
-            for i in range(2):
+                z_acc = psum.tile([P, N], F32, name="z_acc")
                 for t in range(NODE_BLOCKS):
                     nc.tensor.matmul(
-                        z_acc[:, i, :],
-                        h_bf[t][:, i * P : (i + 1) * P],
-                        ahat_t[:, t, :],
-                        start=(t == 0),
-                        stop=(t == NODE_BLOCKS - 1),
+                        z_acc[:], h_bf[t][:], ahat_t[:, t, :], start=(t == 0), stop=(t == NODE_BLOCKS - 1)
                     )
-            half_relu = work.tile([P, 2, N], F32, name="half_relu")
-            nc.scalar.activation(half_relu[:], z_acc[:], ACT.Relu, scale=BETA)
+                half_relu = work.tile([P, N], F32, name="half_relu")
+                nc.scalar.activation(half_relu[:], z_acc[:], ACT.Relu, scale=BETA)
 
-            for i in range(2):
                 nc.vector.tensor_tensor(
-                    windows[q, i][:].indirect(offsets[:]),
-                    x_raw[q][:, i, 0:N],
-                    half_relu[:, i, :],
+                    windows[b][:].indirect(offsets[:]),
+                    x_raw[b // LOAD_BLOCKS][:, b % LOAD_BLOCKS, 0:N],
+                    half_relu[:],
                     mybir.AluOpType.add,
                 )
-                nc.sync.dma_start(out_pairs[q][:, i, :], windows[q, i][:])
+                nc.sync.dma_start(out_blocks[b], windows[b][:])

@@ -9,6 +9,7 @@ CHUNKS = 4
 CHUNK = C // CHUNKS
 CHUNK_BLOCKS = CHUNK // P
 LOADS = 2
+STEPS = CHUNKS * LOADS
 LOAD_BLOCKS = C // (P * LOADS)
 NODE_BLOCKS = U // P
 BLOCKS = C // P
@@ -37,23 +38,20 @@ def tile_structureawaregcn_kernel(tc, base, x, w_gcn, adj, offs, out):
         make_identity(nc, identity[:])
 
         x_raw = [held.tile([P, LOAD_BLOCKS, U], F32, name=f"x_raw{g}") for g in range(LOADS)]
-        w_raw = [
-            [held.tile([P, LOAD_BLOCKS, CHUNK], F32, name=f"w_raw{q}_{g}") for g in range(LOADS)]
-            for q in range(CHUNKS)
-        ]
+        w_raw = [held.tile([P, LOAD_BLOCKS, CHUNK], F32, name=f"w_raw{s}") for s in range(STEPS)]
         windows = [held.tile([P, S], F32, name=f"window{b}") for b in range(BLOCKS)]
         offsets = held.tile([P, N // 16], U16, name="offsets")
         adj_rows = held.tile([P, NODE_BLOCKS, U], F32, name="adj_rows")
 
-        nc.gpsimd.dma_start(adj_rows[:], adj.rearrange("(t p) v -> p t v", p=P))
+        nc.scalar.dma_start(adj_rows[:], adj.rearrange("(t p) v -> p t v", p=P))
         for b in range(BLOCKS // 2):
-            nc.gpsimd.dma_start(windows[b][:], base_blocks[b])
-        for q in range(CHUNKS):
-            for g in range(LOADS):
-                if q == 0:
-                    nc.sync.dma_start(x_raw[g][:], x_loads[g])
-                nc.sync.dma_start(w_raw[q][g][:], w_loads[g][:, :, q * CHUNK : (q + 1) * CHUNK])
+            nc.scalar.dma_start(windows[b][:], base_blocks[b])
+        for s in range(STEPS):
+            q, g = divmod(s, LOADS)
             if q == 0:
+                nc.sync.dma_start(x_raw[g][:], x_loads[g])
+            nc.sync.dma_start(w_raw[s][:], w_loads[g][:, :, q * CHUNK : (q + 1) * CHUNK])
+            if s == LOADS - 1:
                 nc.sync.dma_start(offsets[:], offs)
         for b in range(BLOCKS // 2, BLOCKS):
             nc.sync.dma_start(windows[b][:], base_blocks[b])
@@ -81,39 +79,52 @@ def tile_structureawaregcn_kernel(tc, base, x, w_gcn, adj, offs, out):
             nc.scalar.copy(by_scalar[:], raw[:, half:LOAD_BLOCKS, :])
             return [by_vector[:, b, :] for b in range(half)] + [by_scalar[:, b, :] for b in range(half)]
 
-        x_bf = [cast_load(f"x_bf{g}", x_raw[g]) for g in range(LOADS)]
+        x_bf = {}
+        h_acc = {}
+        half_relu = {}
 
-        for q in range(CHUNKS):
-            h_acc = [psum.tile([P, CHUNK], F32, name=f"h_acc{t}") for t in range(NODE_BLOCKS)]
-            for g in range(LOADS):
-                w_bf = cast_load(f"w_bf{q}_{g}", w_raw[q][g])
-                for b in range(LOAD_BLOCKS):
-                    for t in range(NODE_BLOCKS):
-                        nc.tensor.matmul(
-                            h_acc[t][:],
-                            x_bf[g][b][:, t * P : (t + 1) * P],
-                            w_bf[b],
-                            start=(g == 0 and b == 0),
-                            stop=(g == LOADS - 1 and b == LOAD_BLOCKS - 1),
-                        )
-            for i in range(CHUNK_BLOCKS):
-                b = q * CHUNK_BLOCKS + i
-                h_bf = [work.tile([P, P], BF16, name=f"h_bf{t}") for t in range(NODE_BLOCKS)]
-                nc.vector.tensor_copy(h_bf[0][:], h_acc[0][:, i * P : (i + 1) * P])
-                nc.scalar.copy(h_bf[1][:], h_acc[1][:, i * P : (i + 1) * P])
-
-                z_acc = psum.tile([P, N], F32, name="z_acc")
+        def accumulate(s):
+            q, g = divmod(s, LOADS)
+            if q == 0:
+                x_bf[g] = cast_load(f"x_bf{g}", x_raw[g])
+            if g == 0:
+                h_acc[q] = [psum.tile([P, CHUNK], F32, name=f"h_acc{t}") for t in range(NODE_BLOCKS)]
+            w_bf = cast_load(f"w_bf{s}", w_raw[s])
+            for b in range(LOAD_BLOCKS):
                 for t in range(NODE_BLOCKS):
                     nc.tensor.matmul(
-                        z_acc[:], h_bf[t][:], ahat_t[:, t, :], start=(t == 0), stop=(t == NODE_BLOCKS - 1)
+                        h_acc[q][t][:],
+                        x_bf[g][b][:, t * P : (t + 1) * P],
+                        w_bf[b],
+                        start=(g == 0 and b == 0),
+                        stop=(g == LOADS - 1 and b == LOAD_BLOCKS - 1),
                     )
-                half_relu = work.tile([P, N], F32, name="half_relu")
-                nc.scalar.activation(half_relu[:], z_acc[:], ACT.Relu, scale=BETA)
 
-                nc.vector.tensor_tensor(
-                    windows[b][:].indirect(offsets[:]),
-                    x_raw[b // LOAD_BLOCKS][:, b % LOAD_BLOCKS, 0:N],
-                    half_relu[:],
-                    mybir.AluOpType.add,
-                )
-                nc.sync.dma_start(out_blocks[b], windows[b][:])
+        def aggregate(b):
+            q, i = divmod(b, CHUNK_BLOCKS)
+            h_bf = [work.tile([P, P], BF16, name=f"h_bf{t}") for t in range(NODE_BLOCKS)]
+            nc.vector.tensor_copy(h_bf[0][:], h_acc[q][0][:, i * P : (i + 1) * P])
+            nc.scalar.copy(h_bf[1][:], h_acc[q][1][:, i * P : (i + 1) * P])
+            z_acc = psum.tile([P, N], F32, name="z_acc")
+            for t in range(NODE_BLOCKS):
+                nc.tensor.matmul(z_acc[:], h_bf[t][:], ahat_t[:, t, :], start=(t == 0), stop=(t == NODE_BLOCKS - 1))
+            half_relu[b] = work.tile([P, N], F32, name="half_relu")
+            nc.scalar.activation(half_relu[b][:], z_acc[:], ACT.Relu, scale=BETA)
+
+        def place(b):
+            nc.vector.tensor_tensor(
+                windows[b][:].indirect(offsets[:]),
+                x_raw[b // LOAD_BLOCKS][:, b % LOAD_BLOCKS, 0:N],
+                half_relu[b][:],
+                mybir.AluOpType.add,
+            )
+            nc.sync.dma_start(out_blocks[b], windows[b][:])
+
+        for s in range(STEPS + 3):
+            if s < STEPS:
+                accumulate(s)
+            if LOADS <= s <= STEPS and s % LOADS == 0:
+                for b in range((s // LOADS - 1) * CHUNK_BLOCKS, (s // LOADS) * CHUNK_BLOCKS):
+                    aggregate(b)
+            if 0 <= s - 3 < BLOCKS:
+                place(s - 3)

@@ -5,10 +5,10 @@ P = 128
 C, S, N, U = 1024, 256, 128, 256
 EPS = 1e-8
 BETA = 0.5
-CHUNKS = 4
+CHUNKS = 2
 CHUNK = C // CHUNKS
 CHUNK_BLOCKS = CHUNK // P
-LOADS = 2
+LOADS = 4
 STEPS = CHUNKS * LOADS
 LOAD_BLOCKS = C // (P * LOADS)
 NODE_BLOCKS = U // P
@@ -108,7 +108,7 @@ def tile_structureawaregcn_kernel(tc, base, x, w_gcn, adj, offs, out):
             z_acc = psum.tile([P, N], F32, name="z_acc")
             for t in range(NODE_BLOCKS):
                 nc.tensor.matmul(z_acc[:], h_bf[t][:], ahat_t[:, t, :], start=(t == 0), stop=(t == NODE_BLOCKS - 1))
-            half_relu[b] = work.tile([P, N], F32, name="half_relu")
+            half_relu[b] = held.tile([P, N], F32, name=f"half_relu{b}")
             nc.scalar.activation(half_relu[b][:], z_acc[:], ACT.Relu, scale=BETA)
 
         def place(b):
@@ -120,11 +120,11 @@ def tile_structureawaregcn_kernel(tc, base, x, w_gcn, adj, offs, out):
             )
             nc.sync.dma_start(out_blocks[b], windows[b][:])
 
-        for s in range(STEPS + 3):
+        for s in range(BLOCKS + LOADS + 1):
             if s < STEPS:
                 accumulate(s)
             if LOADS <= s <= STEPS and s % LOADS == 0:
                 for b in range((s // LOADS - 1) * CHUNK_BLOCKS, (s // LOADS) * CHUNK_BLOCKS):
                     aggregate(b)
-            if 0 <= s - 3 < BLOCKS:
-                place(s - 3)
+            if s >= LOADS + 1:
+                place(s - LOADS - 1)

@@ -5,11 +5,13 @@ P = 128
 C, S, N, U = 1024, 256, 128, 256
 EPS = 1e-8
 BETA = 0.5
-CHUNKS = 2
+CHUNKS = 4
 CHUNK = C // CHUNKS
 CHUNK_BLOCKS = CHUNK // P
-LOADS = 4
+LOADS = 2
 STEPS = CHUNKS * LOADS
+CAST_AHEAD = 2
+PLACE_BEHIND = 4
 LOAD_BLOCKS = C // (P * LOADS)
 NODE_BLOCKS = U // P
 BLOCKS = C // P
@@ -44,8 +46,6 @@ def tile_structureawaregcn_kernel(tc, base, x, w_gcn, adj, offs, out):
         adj_rows = held.tile([P, NODE_BLOCKS, U], F32, name="adj_rows")
 
         nc.scalar.dma_start(adj_rows[:], adj.rearrange("(t p) v -> p t v", p=P))
-        for b in range(BLOCKS // 2):
-            nc.scalar.dma_start(windows[b][:], base_blocks[b])
         for s in range(STEPS):
             q, g = divmod(s, LOADS)
             if q == 0:
@@ -53,7 +53,9 @@ def tile_structureawaregcn_kernel(tc, base, x, w_gcn, adj, offs, out):
             nc.sync.dma_start(w_raw[s][:], w_loads[g][:, :, q * CHUNK : (q + 1) * CHUNK])
             if s == LOADS - 1:
                 nc.sync.dma_start(offsets[:], offs)
-        for b in range(BLOCKS // 2, BLOCKS):
+            if s >= STEPS // 2:
+                nc.sync.dma_start(windows[s - STEPS // 2][:], base_blocks[s - STEPS // 2])
+        for b in range(STEPS - STEPS // 2, BLOCKS):
             nc.sync.dma_start(windows[b][:], base_blocks[b])
 
         deg = held.tile([P, NODE_BLOCKS], F32, name="deg")
@@ -80,22 +82,25 @@ def tile_structureawaregcn_kernel(tc, base, x, w_gcn, adj, offs, out):
             return [by_vector[:, b, :] for b in range(half)] + [by_scalar[:, b, :] for b in range(half)]
 
         x_bf = {}
+        w_bf = {}
         h_acc = {}
         half_relu = {}
 
+        def cast(s):
+            if s < LOADS:
+                x_bf[s] = cast_load(f"x_bf{s}", x_raw[s])
+            w_bf[s] = cast_load(f"w_bf{s}", w_raw[s])
+
         def accumulate(s):
             q, g = divmod(s, LOADS)
-            if q == 0:
-                x_bf[g] = cast_load(f"x_bf{g}", x_raw[g])
             if g == 0:
                 h_acc[q] = [psum.tile([P, CHUNK], F32, name=f"h_acc{t}") for t in range(NODE_BLOCKS)]
-            w_bf = cast_load(f"w_bf{s}", w_raw[s])
             for b in range(LOAD_BLOCKS):
                 for t in range(NODE_BLOCKS):
                     nc.tensor.matmul(
                         h_acc[q][t][:],
                         x_bf[g][b][:, t * P : (t + 1) * P],
-                        w_bf[b],
+                        w_bf[s][b],
                         start=(g == 0 and b == 0),
                         stop=(g == LOADS - 1 and b == LOAD_BLOCKS - 1),
                     )
@@ -120,11 +125,15 @@ def tile_structureawaregcn_kernel(tc, base, x, w_gcn, adj, offs, out):
             )
             nc.sync.dma_start(out_blocks[b], windows[b][:])
 
-        for s in range(BLOCKS + LOADS + 1):
+        for s in range(CAST_AHEAD):
+            cast(s)
+        for s in range(BLOCKS + PLACE_BEHIND):
+            if s + CAST_AHEAD < STEPS:
+                cast(s + CAST_AHEAD)
             if s < STEPS:
                 accumulate(s)
             if LOADS <= s <= STEPS and s % LOADS == 0:
                 for b in range((s // LOADS - 1) * CHUNK_BLOCKS, (s // LOADS) * CHUNK_BLOCKS):
                     aggregate(b)
-            if s >= LOADS + 1:
-                place(s - LOADS - 1)
+            if s >= PLACE_BEHIND:
+                place(s - PLACE_BEHIND)

@@ -5,16 +5,16 @@ P = 128
 C, S, N, U = 1024, 256, 128, 256
 EPS = 1e-8
 BETA = 0.5
-CHUNKS = 4
-CHUNK = C // CHUNKS
-CHUNK_BLOCKS = CHUNK // P
-LOADS = 2
-STEPS = CHUNKS * LOADS
-CAST_AHEAD = 2
-PLACE_BEHIND = 4
-LOAD_BLOCKS = C // (P * LOADS)
-NODE_BLOCKS = U // P
 BLOCKS = C // P
+NODE_BLOCKS = U // P
+CHUNK_BLOCKS = (4, 3, 1)
+CHUNKS = len(CHUNK_BLOCKS)
+FIRST_BLOCK = [sum(CHUNK_BLOCKS[:q]) for q in range(CHUNKS)]
+WIDEST = max(CHUNK_BLOCKS)
+GROUP_BLOCKS = 2
+GROUPS = BLOCKS // GROUP_BLOCKS
+STEPS = CHUNKS * GROUPS
+CAST_AHEAD = 2
 FLOPS = 2 * U * C * C + 2 * N * U * C
 
 F32 = mybir.dt.float32
@@ -27,35 +27,40 @@ def tile_structureawaregcn_kernel(tc, base, x, w_gcn, adj, offs, out):
     nc = tc.nc
     base_blocks = base.rearrange("(b p) s -> b p s", p=P)
     out_blocks = out.rearrange("(b p) s -> b p s", p=P)
-    x_loads = x.rearrange("(g b p) u -> g p b u", b=LOAD_BLOCKS, p=P)
-    w_loads = w_gcn.rearrange("(g b p) c -> g p b c", b=LOAD_BLOCKS, p=P)
+    x_groups = x.rearrange("(g b p) u -> g p b u", b=GROUP_BLOCKS, p=P)
+    w_groups = w_gcn.rearrange("(g b p) c -> g p b c", b=GROUP_BLOCKS, p=P)
 
     with (
         tc.tile_pool(name="held", bufs=1) as held,
-        tc.tile_pool(name="work", bufs=4) as work,
         tc.psum_pool(name="psum_once", bufs=1) as psum_once,
         tc.psum_pool(name="psum", bufs=2) as psum,
     ):
         identity = held.tile([P, P], F32, name="identity")
         make_identity(nc, identity[:])
 
-        x_raw = [held.tile([P, LOAD_BLOCKS, U], F32, name=f"x_raw{g}") for g in range(LOADS)]
-        w_raw = [held.tile([P, LOAD_BLOCKS, CHUNK], F32, name=f"w_raw{s}") for s in range(STEPS)]
+        x_raw = [held.tile([P, GROUP_BLOCKS, U], F32, name=f"x_raw{g}") for g in range(GROUPS)]
+        w_raw = [
+            [held.tile([P, GROUP_BLOCKS, CHUNK_BLOCKS[q] * P], F32, name=f"w_raw{q}_{g}") for g in range(GROUPS)]
+            for q in range(CHUNKS)
+        ]
         windows = [held.tile([P, S], F32, name=f"window{b}") for b in range(BLOCKS)]
         offsets = held.tile([P, N // 16], U16, name="offsets")
         adj_rows = held.tile([P, NODE_BLOCKS, U], F32, name="adj_rows")
 
         nc.scalar.dma_start(adj_rows[:], adj.rearrange("(t p) v -> p t v", p=P))
-        for s in range(STEPS):
-            q, g = divmod(s, LOADS)
+        for q in range(CHUNKS):
+            first_column = FIRST_BLOCK[q] * P
+            for g in range(GROUPS):
+                if q == 0:
+                    nc.sync.dma_start(x_raw[g][:], x_groups[g])
+                nc.sync.dma_start(
+                    w_raw[q][g][:], w_groups[g][:, :, first_column : first_column + CHUNK_BLOCKS[q] * P]
+                )
+                if q == 1:
+                    nc.sync.dma_start(windows[g][:], base_blocks[g])
             if q == 0:
-                nc.sync.dma_start(x_raw[g][:], x_loads[g])
-            nc.sync.dma_start(w_raw[s][:], w_loads[g][:, :, q * CHUNK : (q + 1) * CHUNK])
-            if s == LOADS - 1:
                 nc.sync.dma_start(offsets[:], offs)
-            if s >= STEPS // 2:
-                nc.sync.dma_start(windows[s - STEPS // 2][:], base_blocks[s - STEPS // 2])
-        for b in range(STEPS - STEPS // 2, BLOCKS):
+        for b in range(GROUPS, BLOCKS):
             nc.sync.dma_start(windows[b][:], base_blocks[b])
 
         deg = held.tile([P, NODE_BLOCKS], F32, name="deg")
@@ -73,13 +78,12 @@ def tile_structureawaregcn_kernel(tc, base, x, w_gcn, adj, offs, out):
             nc.vector.tensor_scalar_mul(ahat_t[:, t, :], flipped[:, t, :], d[:, t : t + 1])
 
         def cast_load(name, raw):
-            half = LOAD_BLOCKS // 2
             width = raw.shape[2]
-            by_vector = held.tile([P, half, width], BF16, name=f"{name}_v")
-            by_scalar = held.tile([P, half, width], BF16, name=f"{name}_s")
-            nc.vector.tensor_copy(by_vector[:], raw[:, 0:half, :])
-            nc.scalar.copy(by_scalar[:], raw[:, half:LOAD_BLOCKS, :])
-            return [by_vector[:, b, :] for b in range(half)] + [by_scalar[:, b, :] for b in range(half)]
+            by_vector = held.tile([P, width], BF16, name=f"{name}_v")
+            by_scalar = held.tile([P, width], BF16, name=f"{name}_s")
+            nc.vector.tensor_copy(by_vector[:], raw[:, 0, :])
+            nc.scalar.copy(by_scalar[:], raw[:, 1, :])
+            return [by_vector[:], by_scalar[:]]
 
         x_bf = {}
         w_bf = {}
@@ -87,53 +91,64 @@ def tile_structureawaregcn_kernel(tc, base, x, w_gcn, adj, offs, out):
         half_relu = {}
 
         def cast(s):
-            if s < LOADS:
-                x_bf[s] = cast_load(f"x_bf{s}", x_raw[s])
-            w_bf[s] = cast_load(f"w_bf{s}", w_raw[s])
+            q, g = divmod(s, GROUPS)
+            if q == 0:
+                x_bf[g] = cast_load(f"x_bf{g}", x_raw[g])
+            w_bf[s] = cast_load(f"w_bf{s}", w_raw[q][g])
 
         def accumulate(s):
-            q, g = divmod(s, LOADS)
+            q, g = divmod(s, GROUPS)
+            width = CHUNK_BLOCKS[q] * P
             if g == 0:
-                h_acc[q] = [psum.tile([P, CHUNK], F32, name=f"h_acc{t}") for t in range(NODE_BLOCKS)]
-            for b in range(LOAD_BLOCKS):
+                h_acc[q] = [psum.tile([P, WIDEST * P], F32, name=f"h_acc{t}") for t in range(NODE_BLOCKS)]
+            for b in range(GROUP_BLOCKS):
                 for t in range(NODE_BLOCKS):
                     nc.tensor.matmul(
-                        h_acc[q][t][:],
+                        h_acc[q][t][:, 0:width],
                         x_bf[g][b][:, t * P : (t + 1) * P],
                         w_bf[s][b],
                         start=(g == 0 and b == 0),
-                        stop=(g == LOADS - 1 and b == LOAD_BLOCKS - 1),
+                        stop=(g == GROUPS - 1 and b == GROUP_BLOCKS - 1),
                     )
 
-        def aggregate(b):
-            q, i = divmod(b, CHUNK_BLOCKS)
-            h_bf = [work.tile([P, P], BF16, name=f"h_bf{t}") for t in range(NODE_BLOCKS)]
-            nc.vector.tensor_copy(h_bf[0][:], h_acc[q][0][:, i * P : (i + 1) * P])
-            nc.scalar.copy(h_bf[1][:], h_acc[q][1][:, i * P : (i + 1) * P])
-            z_acc = psum.tile([P, N], F32, name="z_acc")
-            for t in range(NODE_BLOCKS):
-                nc.tensor.matmul(z_acc[:], h_bf[t][:], ahat_t[:, t, :], start=(t == 0), stop=(t == NODE_BLOCKS - 1))
-            half_relu[b] = held.tile([P, N], F32, name=f"half_relu{b}")
-            nc.scalar.activation(half_relu[b][:], z_acc[:], ACT.Relu, scale=BETA)
+        def aggregate(q):
+            width = CHUNK_BLOCKS[q] * P
+            h_bf = [held.tile([P, width], BF16, name=f"h_bf{q}_{t}") for t in range(NODE_BLOCKS)]
+            nc.vector.tensor_copy(h_bf[0][:], h_acc[q][0][:, 0:width])
+            nc.scalar.copy(h_bf[1][:], h_acc[q][1][:, 0:width])
+            z_acc = psum.tile([P, WIDEST, N], F32, name="z_acc")
+            for i in range(CHUNK_BLOCKS[q]):
+                for t in range(NODE_BLOCKS):
+                    nc.tensor.matmul(
+                        z_acc[:, i, :],
+                        h_bf[t][:, i * P : (i + 1) * P],
+                        ahat_t[:, t, :],
+                        start=(t == 0),
+                        stop=(t == NODE_BLOCKS - 1),
+                    )
+            half_relu[q] = held.tile([P, CHUNK_BLOCKS[q], N], F32, name=f"half_relu{q}")
+            nc.scalar.activation(half_relu[q][:], z_acc[:, 0 : CHUNK_BLOCKS[q], :], ACT.Relu, scale=BETA)
 
-        def place(b):
+        def place(q, i):
+            b = FIRST_BLOCK[q] + i
             nc.vector.tensor_tensor(
                 windows[b][:].indirect(offsets[:]),
-                x_raw[b // LOAD_BLOCKS][:, b % LOAD_BLOCKS, 0:N],
-                half_relu[b][:],
+                x_raw[b // GROUP_BLOCKS][:, b % GROUP_BLOCKS, 0:N],
+                half_relu[q][:, i, :],
                 mybir.AluOpType.add,
             )
             nc.sync.dma_start(out_blocks[b], windows[b][:])
 
         for s in range(CAST_AHEAD):
             cast(s)
-        for s in range(BLOCKS + PLACE_BEHIND):
+        for s in range(STEPS + 1 + CHUNK_BLOCKS[-1]):
             if s + CAST_AHEAD < STEPS:
                 cast(s + CAST_AHEAD)
             if s < STEPS:
                 accumulate(s)
-            if LOADS <= s <= STEPS and s % LOADS == 0:
-                for b in range((s // LOADS - 1) * CHUNK_BLOCKS, (s // LOADS) * CHUNK_BLOCKS):
-                    aggregate(b)
-            if s >= PLACE_BEHIND:
-                place(s - PLACE_BEHIND)
+            for q in range(CHUNKS):
+                since_complete = s - (q + 1) * GROUPS
+                if since_complete == 0:
+                    aggregate(q)
+                if 1 <= since_complete <= CHUNK_BLOCKS[q]:
+                    place(q, since_complete - 1)

@@ -7,14 +7,14 @@ EPS = 1e-8
 BETA = 0.5
 BLOCKS = C // P
 NODE_BLOCKS = U // P
-CHUNK_BLOCKS = (4, 3, 1)
+CHUNK_BLOCKS = (3, 3, 2)
 CHUNKS = len(CHUNK_BLOCKS)
 FIRST_BLOCK = [sum(CHUNK_BLOCKS[:q]) for q in range(CHUNKS)]
 WIDEST = max(CHUNK_BLOCKS)
 GROUP_BLOCKS = 2
 GROUPS = BLOCKS // GROUP_BLOCKS
 STEPS = CHUNKS * GROUPS
-CAST_AHEAD = 2
+CAST_AHEAD = 3
 FLOPS = 2 * U * C * C + 2 * N * U * C
 
 F32 = mybir.dt.float32
@@ -56,7 +56,7 @@ def tile_structureawaregcn_kernel(tc, base, x, w_gcn, adj, offs, out):
                 nc.sync.dma_start(
                     w_raw[q][g][:], w_groups[g][:, :, first_column : first_column + CHUNK_BLOCKS[q] * P]
                 )
-                if q == 1:
+                if q == CHUNKS - 1:
                     nc.sync.dma_start(windows[g][:], base_blocks[g])
             if q == 0:
                 nc.sync.dma_start(offsets[:], offs)
@@ -77,7 +77,7 @@ def tile_structureawaregcn_kernel(tc, base, x, w_gcn, adj, offs, out):
             nc.tensor.transpose(flipped[:, t, :], scaled_rows[:, t * P : (t + 1) * P], identity[:])
             nc.vector.tensor_scalar_mul(ahat_t[:, t, :], flipped[:, t, :], d[:, t : t + 1])
 
-        def cast_load(name, raw):
+        def cast_shared(name, raw):
             width = raw.shape[2]
             by_vector = held.tile([P, width], BF16, name=f"{name}_v")
             by_scalar = held.tile([P, width], BF16, name=f"{name}_s")
@@ -93,8 +93,8 @@ def tile_structureawaregcn_kernel(tc, base, x, w_gcn, adj, offs, out):
         def cast(s):
             q, g = divmod(s, GROUPS)
             if q == 0:
-                x_bf[g] = cast_load(f"x_bf{g}", x_raw[g])
-            w_bf[s] = cast_load(f"w_bf{s}", w_raw[q][g])
+                x_bf[g] = cast_shared(f"x_bf{g}", x_raw[g])
+            w_bf[s] = cast_shared(f"w_bf{s}", w_raw[q][g])
 
         def accumulate(s):
             q, g = divmod(s, GROUPS)
@@ -112,29 +112,32 @@ def tile_structureawaregcn_kernel(tc, base, x, w_gcn, adj, offs, out):
                     )
 
         def aggregate(q):
-            width = CHUNK_BLOCKS[q] * P
-            h_bf = [held.tile([P, width], BF16, name=f"h_bf{q}_{t}") for t in range(NODE_BLOCKS)]
-            nc.vector.tensor_copy(h_bf[0][:], h_acc[q][0][:, 0:width])
-            nc.scalar.copy(h_bf[1][:], h_acc[q][1][:, 0:width])
-            z_acc = psum.tile([P, WIDEST, N], F32, name="z_acc")
             for i in range(CHUNK_BLOCKS[q]):
+                b = FIRST_BLOCK[q] + i
+                h_bf = [held.tile([P, P], BF16, name=f"h_bf{b}_{t}") for t in range(NODE_BLOCKS)]
+                if q == 0:
+                    nc.vector.tensor_copy(h_bf[0][:], h_acc[q][0][:, i * P : (i + 1) * P])
+                else:
+                    nc.scalar.copy(h_bf[0][:], h_acc[q][0][:, i * P : (i + 1) * P])
+                nc.scalar.copy(h_bf[1][:], h_acc[q][1][:, i * P : (i + 1) * P])
+                z_acc = psum.tile([P, N], F32, name="z_acc")
                 for t in range(NODE_BLOCKS):
                     nc.tensor.matmul(
-                        z_acc[:, i, :],
-                        h_bf[t][:, i * P : (i + 1) * P],
+                        z_acc[:],
+                        h_bf[t][:],
                         ahat_t[:, t, :],
                         start=(t == 0),
                         stop=(t == NODE_BLOCKS - 1),
                     )
-            half_relu[q] = held.tile([P, CHUNK_BLOCKS[q], N], F32, name=f"half_relu{q}")
-            nc.scalar.activation(half_relu[q][:], z_acc[:, 0 : CHUNK_BLOCKS[q], :], ACT.Relu, scale=BETA)
+                half_relu[b] = held.tile([P, N], F32, name=f"half_relu{b}")
+                nc.scalar.activation(half_relu[b][:], z_acc[:], ACT.Relu, scale=BETA)
 
         def place(q, i):
             b = FIRST_BLOCK[q] + i
             nc.vector.tensor_tensor(
                 windows[b][:].indirect(offsets[:]),
                 x_raw[b // GROUP_BLOCKS][:, b % GROUP_BLOCKS, 0:N],
-                half_relu[q][:, i, :],
+                half_relu[b][:],
                 mybir.AluOpType.add,
             )
             nc.sync.dma_start(out_blocks[b], windows[b][:])

@@ -34,6 +34,7 @@ def tile_structureawaregcn_kernel(tc, base, x, w_gcn, adj, offs, out):
         tc.tile_pool(name="held", bufs=1) as held,
         tc.psum_pool(name="psum_once", bufs=1) as psum_once,
         tc.psum_pool(name="psum", bufs=2) as psum,
+        tc.psum_pool(name="psum_z", bufs=WIDEST) as psum_z,
     ):
         identity = held.tile([P, P], F32, name="identity")
         make_identity(nc, identity[:])
@@ -112,25 +113,28 @@ def tile_structureawaregcn_kernel(tc, base, x, w_gcn, adj, offs, out):
                     )
 
         def aggregate(q):
-            for i in range(CHUNK_BLOCKS[q]):
-                b = FIRST_BLOCK[q] + i
-                h_bf = [held.tile([P, P], BF16, name=f"h_bf{b}_{t}") for t in range(NODE_BLOCKS)]
+            blocks = range(CHUNK_BLOCKS[q])
+            h_bf = [[held.tile([P, P], BF16, name=f"h_bf{q}_{i}_{t}") for t in range(NODE_BLOCKS)] for i in blocks]
+            for i in blocks:
                 if q == 0:
-                    nc.vector.tensor_copy(h_bf[0][:], h_acc[q][0][:, i * P : (i + 1) * P])
+                    nc.vector.tensor_copy(h_bf[i][0][:], h_acc[q][0][:, i * P : (i + 1) * P])
                 else:
-                    nc.scalar.copy(h_bf[0][:], h_acc[q][0][:, i * P : (i + 1) * P])
-                nc.scalar.copy(h_bf[1][:], h_acc[q][1][:, i * P : (i + 1) * P])
-                z_acc = psum.tile([P, N], F32, name="z_acc")
-                for t in range(NODE_BLOCKS):
+                    nc.scalar.copy(h_bf[i][0][:], h_acc[q][0][:, i * P : (i + 1) * P])
+                nc.scalar.copy(h_bf[i][1][:], h_acc[q][1][:, i * P : (i + 1) * P])
+            z_acc = [psum_z.tile([P, N], F32, name="z_acc") for i in blocks]
+            for t in range(NODE_BLOCKS):
+                for i in blocks:
                     nc.tensor.matmul(
-                        z_acc[:],
-                        h_bf[t][:],
+                        z_acc[i][:],
+                        h_bf[i][t][:],
                         ahat_t[:, t, :],
                         start=(t == 0),
                         stop=(t == NODE_BLOCKS - 1),
                     )
+            for i in blocks:
+                b = FIRST_BLOCK[q] + i
                 half_relu[b] = held.tile([P, N], F32, name=f"half_relu{b}")
-                nc.scalar.activation(half_relu[b][:], z_acc[:], ACT.Relu, scale=BETA)
+                nc.scalar.activation(half_relu[b][:], z_acc[i][:], ACT.Relu, scale=BETA)
 
         def place(q, i):
             b = FIRST_BLOCK[q] + i

@@ -7,10 +7,11 @@ EPS = 1e-8
 BETA = 0.5
 BLOCKS = C // P
 NODE_BLOCKS = U // P
-CHUNK_BLOCKS = (3, 3, 2)
+CHUNK_BLOCKS = (2, 4, 2)
 CHUNKS = len(CHUNK_BLOCKS)
 FIRST_BLOCK = [sum(CHUNK_BLOCKS[:q]) for q in range(CHUNKS)]
 WIDEST = max(CHUNK_BLOCKS)
+PAIR = 2
 GROUP_BLOCKS = 2
 GROUPS = BLOCKS // GROUP_BLOCKS
 STEPS = CHUNKS * GROUPS
@@ -32,9 +33,8 @@ def tile_structureawaregcn_kernel(tc, base, x, w_gcn, adj, offs, out):
 
     with (
         tc.tile_pool(name="held", bufs=1) as held,
-        tc.psum_pool(name="psum_once", bufs=1) as psum_once,
         tc.psum_pool(name="psum", bufs=2) as psum,
-        tc.psum_pool(name="psum_z", bufs=WIDEST) as psum_z,
+        tc.psum_pool(name="psum_z", bufs=2 * PAIR) as psum_z,
     ):
         identity = held.tile([P, P], F32, name="identity")
         make_identity(nc, identity[:])
@@ -72,7 +72,7 @@ def tile_structureawaregcn_kernel(tc, base, x, w_gcn, adj, offs, out):
         nc.vector.reciprocal(d[:], root[:])
         scaled_rows = held.tile([P, U], F32, name="scaled_rows")
         nc.vector.tensor_scalar_mul(scaled_rows[:], adj_rows[:, 0, :], d[:, 0:1])
-        flipped = psum_once.tile([P, NODE_BLOCKS, N], F32, name="flipped")
+        flipped = psum_z.tile([P, NODE_BLOCKS, N], F32, name="flipped", tag="z_acc")
         ahat_t = held.tile([P, NODE_BLOCKS, N], BF16, name="ahat_t")
         for t in range(NODE_BLOCKS):
             nc.tensor.transpose(flipped[:, t, :], scaled_rows[:, t * P : (t + 1) * P], identity[:])
@@ -113,15 +113,18 @@ def tile_structureawaregcn_kernel(tc, base, x, w_gcn, adj, offs, out):
                     )
 
         def aggregate(q):
-            blocks = range(CHUNK_BLOCKS[q])
-            h_bf = [[held.tile([P, P], BF16, name=f"h_bf{q}_{i}_{t}") for t in range(NODE_BLOCKS)] for i in blocks]
+            for first in range(0, CHUNK_BLOCKS[q], PAIR):
+                aggregate_pair(q, range(first, first + PAIR))
+
+        def aggregate_pair(q, blocks):
+            h_bf = {i: [held.tile([P, P], BF16, name=f"h_bf{q}_{i}_{t}") for t in range(NODE_BLOCKS)] for i in blocks}
             for i in blocks:
                 if q == 0:
                     nc.vector.tensor_copy(h_bf[i][0][:], h_acc[q][0][:, i * P : (i + 1) * P])
                 else:
                     nc.scalar.copy(h_bf[i][0][:], h_acc[q][0][:, i * P : (i + 1) * P])
                 nc.scalar.copy(h_bf[i][1][:], h_acc[q][1][:, i * P : (i + 1) * P])
-            z_acc = [psum_z.tile([P, N], F32, name="z_acc") for i in blocks]
+            z_acc = {i: psum_z.tile([P, N], F32, name="z_acc") for i in blocks}
             for t in range(NODE_BLOCKS):
                 for i in blocks:
                     nc.tensor.matmul(

@@ -78,13 +78,13 @@ def tile_structureawaregcn_kernel(tc, base, x, w_gcn, adj, offs, out):
             nc.tensor.transpose(flipped[:, t, :], scaled_rows[:, t * P : (t + 1) * P], identity[:])
             nc.vector.tensor_scalar_mul(ahat_t[:, t, :], flipped[:, t, :], d[:, t : t + 1])
 
-        def cast_shared(name, raw):
+        def cast_shared(name, raw, first_engine):
             width = raw.shape[2]
-            by_vector = held.tile([P, width], BF16, name=f"{name}_v")
+            by_first = held.tile([P, width], BF16, name=f"{name}_f")
             by_scalar = held.tile([P, width], BF16, name=f"{name}_s")
-            nc.vector.tensor_copy(by_vector[:], raw[:, 0, :])
+            first_engine.tensor_copy(by_first[:], raw[:, 0, :])
             nc.scalar.copy(by_scalar[:], raw[:, 1, :])
-            return [by_vector[:], by_scalar[:]]
+            return [by_first[:], by_scalar[:]]
 
         x_bf = {}
         w_bf = {}
@@ -94,8 +94,8 @@ def tile_structureawaregcn_kernel(tc, base, x, w_gcn, adj, offs, out):
         def cast(s):
             q, g = divmod(s, GROUPS)
             if q == 0:
-                x_bf[g] = cast_shared(f"x_bf{g}", x_raw[g])
-            w_bf[s] = cast_shared(f"w_bf{s}", w_raw[q][g])
+                x_bf[g] = cast_shared(f"x_bf{g}", x_raw[g], nc.vector)
+            w_bf[s] = cast_shared(f"w_bf{s}", w_raw[q][g], nc.vector if q < CHUNKS - 1 else nc.gpsimd)
 
         def accumulate(s):
             q, g = divmod(s, GROUPS)

@@ -26,10 +26,10 @@ ACT = mybir.ActivationFunctionType
 
 def tile_structureawaregcn_kernel(tc, base, x, w_gcn, adj, offs, out):
     nc = tc.nc
-    base_blocks = base.rearrange("(b p) s -> b p s", p=P)
-    out_blocks = out.rearrange("(b p) s -> b p s", p=P)
-    x_groups = x.rearrange("(g b p) u -> g p b u", b=GROUP_BLOCKS, p=P)
-    w_groups = w_gcn.rearrange("(g b p) c -> g p b c", b=GROUP_BLOCKS, p=P)
+    base_blocks = base.rearrange("(g p i) s -> g i p s", i=GROUP_BLOCKS, p=P)
+    out_blocks = out.rearrange("(g p i) s -> g i p s", i=GROUP_BLOCKS, p=P)
+    x_groups = x.rearrange("(g p i) u -> g p i u", i=GROUP_BLOCKS, p=P)
+    w_groups = w_gcn.rearrange("(g p i) c -> g p i c", i=GROUP_BLOCKS, p=P)
 
     with (
         tc.tile_pool(name="held", bufs=1) as held,
@@ -58,11 +58,11 @@ def tile_structureawaregcn_kernel(tc, base, x, w_gcn, adj, offs, out):
                     w_raw[q][g][:], w_groups[g][:, :, first_column : first_column + CHUNK_BLOCKS[q] * P]
                 )
                 if q == CHUNKS - 1:
-                    nc.sync.dma_start(windows[g][:], base_blocks[g])
+                    nc.sync.dma_start(windows[g][:], base_blocks[g // GROUP_BLOCKS][g % GROUP_BLOCKS])
             if q == 0:
                 nc.sync.dma_start(offsets[:], offs)
         for b in range(GROUPS, BLOCKS):
-            nc.sync.dma_start(windows[b][:], base_blocks[b])
+            nc.sync.dma_start(windows[b][:], base_blocks[b // GROUP_BLOCKS][b % GROUP_BLOCKS])
 
         deg = held.tile([P, NODE_BLOCKS], F32, name="deg")
         nc.vector.reduce_sum(deg[:], adj_rows[:], axis=mybir.AxisListType.X)
@@ -119,11 +119,13 @@ def tile_structureawaregcn_kernel(tc, base, x, w_gcn, adj, offs, out):
         def aggregate_pair(q, blocks):
             h_bf = {i: [held.tile([P, P], BF16, name=f"h_bf{q}_{i}_{t}") for t in range(NODE_BLOCKS)] for i in blocks}
             for i in blocks:
+                first = (i // GROUP_BLOCKS) * GROUP_BLOCKS * P + i % GROUP_BLOCKS
+                columns = slice(first, first + GROUP_BLOCKS * (P - 1) + 1, GROUP_BLOCKS)
                 if q == 0:
-                    nc.vector.tensor_copy(h_bf[i][0][:], h_acc[q][0][:, i * P : (i + 1) * P])
+                    nc.vector.tensor_copy(h_bf[i][0][:], h_acc[q][0][:, columns])
                 else:
-                    nc.scalar.copy(h_bf[i][0][:], h_acc[q][0][:, i * P : (i + 1) * P])
-                nc.scalar.copy(h_bf[i][1][:], h_acc[q][1][:, i * P : (i + 1) * P])
+                    nc.scalar.copy(h_bf[i][0][:], h_acc[q][0][:, columns])
+                nc.scalar.copy(h_bf[i][1][:], h_acc[q][1][:, columns])
             z_acc = {i: psum_z.tile([P, N], F32, name="z_acc") for i in blocks}
             for t in range(NODE_BLOCKS):
                 for i in blocks:
@@ -147,7 +149,7 @@ def tile_structureawaregcn_kernel(tc, base, x, w_gcn, adj, offs, out):
                 half_relu[b][:],
                 mybir.AluOpType.add,
             )
-            nc.sync.dma_start(out_blocks[b], windows[b][:])
+            nc.sync.dma_start(out_blocks[b // GROUP_BLOCKS][b % GROUP_BLOCKS], windows[b][:])
 
         for s in range(CAST_AHEAD):
             cast(s)

@@ -48,7 +48,6 @@ def tile_structureawaregcn_kernel(tc, base, x, w_gcn, adj, offs, out):
         offsets = held.tile([P, N // 16], U16, name="offsets")
         adj_rows = held.tile([P, NODE_BLOCKS, U], F32, name="adj_rows")
 
-        nc.scalar.dma_start(adj_rows[:], adj.rearrange("(t p) v -> p t v", p=P))
         for q in range(CHUNKS):
             first_column = FIRST_BLOCK[q] * P
             for g in range(GROUPS):
@@ -59,15 +58,21 @@ def tile_structureawaregcn_kernel(tc, base, x, w_gcn, adj, offs, out):
                 )
                 if q == CHUNKS - 1:
                     nc.sync.dma_start(windows[g][:], base_blocks[g // GROUP_BLOCKS][g % GROUP_BLOCKS])
+                if q == 0 and g == 0:
+                    nc.sync.dma_start(adj_rows[:], adj.rearrange("(t p) v -> p t v", p=P))
             if q == 0:
                 nc.sync.dma_start(offsets[:], offs)
         for b in range(GROUPS, BLOCKS):
             nc.sync.dma_start(windows[b][:], base_blocks[b // GROUP_BLOCKS][b % GROUP_BLOCKS])
 
+        eps = held.tile([P, 1], F32, name="eps")
+        nc.vector.memset(eps[:], EPS)
+        root_eps = held.tile([P, 1], F32, name="root_eps")
+        nc.scalar.activation(root_eps[:], eps[:], ACT.Sqrt)
         deg = held.tile([P, NODE_BLOCKS], F32, name="deg")
         nc.vector.reduce_sum(deg[:], adj_rows[:], axis=mybir.AxisListType.X)
         root = held.tile([P, NODE_BLOCKS], F32, name="root")
-        nc.scalar.activation(root[:], deg[:], ACT.Sqrt, bias=EPS)
+        nc.scalar.activation(root[:], deg[:], ACT.Sqrt, bias=eps[:])
         d = held.tile([P, NODE_BLOCKS], F32, name="d")
         nc.vector.reciprocal(d[:], root[:])
         scaled_rows = held.tile([P, U], F32, name="scaled_rows")

@@ -7,7 +7,7 @@ EPS = 1e-8
 BETA = 0.5
 BLOCKS = C // P
 NODE_BLOCKS = U // P
-CHUNK_BLOCKS = (2, 4, 2)
+CHUNK_BLOCKS = (4, 2, 2)
 CHUNKS = len(CHUNK_BLOCKS)
 FIRST_BLOCK = [sum(CHUNK_BLOCKS[:q]) for q in range(CHUNKS)]
 WIDEST = max(CHUNK_BLOCKS)

@@ -14,7 +14,17 @@ WIDEST = max(CHUNK_BLOCKS)
 PAIR = 2
 GROUP_BLOCKS = 2
 GROUPS = BLOCKS // GROUP_BLOCKS
-STEPS = CHUNKS * GROUPS
+HALF = GROUPS // 2
+FIRST_GROUPS = range(HALF)
+LAST_GROUPS = range(HALF, GROUPS)
+LOADS = (
+    [(g, (0,)) for g in range(GROUPS)]
+    + [(g, (1,)) for g in FIRST_GROUPS]
+    + [(g, (1, 2)) for g in LAST_GROUPS]
+    + [(g, (2,)) for g in FIRST_GROUPS]
+)
+FIRST_BASE_LOAD = GROUPS + HALF
+STEPS = [(q, g) for q in range(CHUNKS) for g, chunks in LOADS if q in chunks]
 CAST_AHEAD = 3
 FLOPS = 2 * U * C * C + 2 * N * U * C
 
@@ -40,30 +50,28 @@ def tile_structureawaregcn_kernel(tc, base, x, w_gcn, adj, offs, out):
         make_identity(nc, identity[:])
 
         x_raw = [held.tile([P, GROUP_BLOCKS, U], F32, name=f"x_raw{g}") for g in range(GROUPS)]
-        w_raw = [
-            [held.tile([P, GROUP_BLOCKS, CHUNK_BLOCKS[q] * P], F32, name=f"w_raw{q}_{g}") for g in range(GROUPS)]
-            for q in range(CHUNKS)
-        ]
+        first_column = [FIRST_BLOCK[chunks[0]] * P for g, chunks in LOADS]
+        width = [sum(CHUNK_BLOCKS[q] for q in chunks) * P for g, chunks in LOADS]
+        w_raw = [held.tile([P, GROUP_BLOCKS, width[n]], F32, name=f"w_raw{n}") for n in range(len(LOADS))]
         windows = [held.tile([P, S], F32, name=f"window{b}") for b in range(BLOCKS)]
         offsets = held.tile([P, N // 16], U16, name="offsets")
         adj_rows = held.tile([P, NODE_BLOCKS, U], F32, name="adj_rows")
 
-        for q in range(CHUNKS):
-            first_column = FIRST_BLOCK[q] * P
-            for g in range(GROUPS):
-                if q == 0:
-                    nc.sync.dma_start(x_raw[g][:], x_groups[g])
-                nc.sync.dma_start(
-                    w_raw[q][g][:], w_groups[g][:, :, first_column : first_column + CHUNK_BLOCKS[q] * P]
-                )
-                if q == CHUNKS - 1:
-                    nc.sync.dma_start(windows[g][:], base_blocks[g // GROUP_BLOCKS][g % GROUP_BLOCKS])
-                if q == 0 and g == 0:
-                    nc.sync.dma_start(adj_rows[:], adj.rearrange("(t p) v -> p t v", p=P))
-            if q == 0:
-                nc.sync.dma_start(offsets[:], offs)
-        for b in range(GROUPS, BLOCKS):
+        def load_base(b):
             nc.sync.dma_start(windows[b][:], base_blocks[b // GROUP_BLOCKS][b % GROUP_BLOCKS])
+
+        for n, (g, chunks) in enumerate(LOADS):
+            if n < GROUPS:
+                nc.sync.dma_start(x_raw[g][:], x_groups[g])
+            nc.sync.dma_start(w_raw[n][:], w_groups[g][:, :, first_column[n] : first_column[n] + width[n]])
+            if n == 0:
+                nc.sync.dma_start(adj_rows[:], adj.rearrange("(t p) v -> p t v", p=P))
+            if n == GROUPS - 1:
+                nc.sync.dma_start(offsets[:], offs)
+            if n >= FIRST_BASE_LOAD:
+                load_base(n - FIRST_BASE_LOAD)
+        for b in range(len(LOADS) - FIRST_BASE_LOAD, BLOCKS):
+            load_base(b)
 
         eps = held.tile([P, 1], F32, name="eps")
         nc.vector.memset(eps[:], EPS)
@@ -96,25 +104,30 @@ def tile_structureawaregcn_kernel(tc, base, x, w_gcn, adj, offs, out):
         h_acc = {}
         half_relu = {}
 
-        def cast(s):
-            q, g = divmod(s, GROUPS)
-            if q == 0:
+        def cast(n):
+            g, chunks = LOADS[n]
+            if n < GROUPS:
                 x_bf[g] = cast_shared(f"x_bf{g}", x_raw[g], nc.vector)
-            w_bf[s] = cast_shared(f"w_bf{s}", w_raw[q][g], nc.vector if q < CHUNKS - 1 else nc.gpsimd)
+            blocks = cast_shared(f"w_bf{n}", w_raw[n], nc.vector if n <= FIRST_BASE_LOAD else nc.gpsimd)
+            for q in chunks:
+                first = FIRST_BLOCK[q] * P - first_column[n]
+                w_bf[q, g] = [block[:, first : first + CHUNK_BLOCKS[q] * P] for block in blocks]
 
         def accumulate(s):
-            q, g = divmod(s, GROUPS)
-            width = CHUNK_BLOCKS[q] * P
-            if g == 0:
+            q, g = STEPS[s]
+            chunk_width = CHUNK_BLOCKS[q] * P
+            first_group = s % GROUPS == 0
+            last_group = s % GROUPS == GROUPS - 1
+            if first_group:
                 h_acc[q] = [psum.tile([P, WIDEST * P], F32, name=f"h_acc{t}") for t in range(NODE_BLOCKS)]
             for b in range(GROUP_BLOCKS):
                 for t in range(NODE_BLOCKS):
                     nc.tensor.matmul(
-                        h_acc[q][t][:, 0:width],
+                        h_acc[q][t][:, 0:chunk_width],
                         x_bf[g][b][:, t * P : (t + 1) * P],
-                        w_bf[s][b],
-                        start=(g == 0 and b == 0),
-                        stop=(g == GROUPS - 1 and b == GROUP_BLOCKS - 1),
+                        w_bf[q, g][b],
+                        start=(first_group and b == 0),
+                        stop=(last_group and b == GROUP_BLOCKS - 1),
                     )
 
         def aggregate(q):
@@ -156,12 +169,12 @@ def tile_structureawaregcn_kernel(tc, base, x, w_gcn, adj, offs, out):
             )
             nc.sync.dma_start(out_blocks[b // GROUP_BLOCKS][b % GROUP_BLOCKS], windows[b][:])
 
-        for s in range(CAST_AHEAD):
-            cast(s)
-        for s in range(STEPS + 1 + CHUNK_BLOCKS[-1]):
-            if s + CAST_AHEAD < STEPS:
+        for n in range(CAST_AHEAD):
+            cast(n)
+        for s in range(len(STEPS) + 1 + CHUNK_BLOCKS[-1]):
+            if s + CAST_AHEAD < len(LOADS):
                 cast(s + CAST_AHEAD)
-            if s < STEPS:
+            if s < len(STEPS):
                 accumulate(s)
             for q in range(CHUNKS):
                 since_complete = s - (q + 1) * GROUPS

import concourse.mybir as mybir
from concourse.masks import make_identity

P = 128
C, S, N, U = 1024, 256, 128, 256
EPS = 1e-8
BETA = 0.5
BLOCKS = C // P
NODE_BLOCKS = U // P
CHUNK_BLOCKS = (4, 2, 2)
CHUNKS = len(CHUNK_BLOCKS)
FIRST_BLOCK = [sum(CHUNK_BLOCKS[:q]) for q in range(CHUNKS)]
WIDEST = max(CHUNK_BLOCKS)
PAIR = 2
GROUP_BLOCKS = 2
GROUPS = BLOCKS // GROUP_BLOCKS
HALF = GROUPS // 2
FIRST_GROUPS = range(HALF)
LAST_GROUPS = range(HALF, GROUPS)
LOADS = (
    [(g, (0,)) for g in range(GROUPS)]
    + [(g, (1,)) for g in FIRST_GROUPS]
    + [(g, (1, 2)) for g in LAST_GROUPS]
    + [(g, (2,)) for g in FIRST_GROUPS]
)
FIRST_BASE_LOAD = GROUPS + HALF
STEPS = [(q, g) for q in range(CHUNKS) for g, chunks in LOADS if q in chunks]
CAST_AHEAD = 3
FLOPS = 2 * U * C * C + 2 * N * U * C

F32 = mybir.dt.float32
BF16 = mybir.dt.bfloat16
U16 = mybir.dt.uint16
ACT = mybir.ActivationFunctionType


def tile_structureawaregcn_kernel(tc, base, x, w_gcn, adj, offs, out):
    nc = tc.nc
    base_blocks = base.rearrange("(g p i) s -> g i p s", i=GROUP_BLOCKS, p=P)
    out_blocks = out.rearrange("(g p i) s -> g i p s", i=GROUP_BLOCKS, p=P)
    x_groups = x.rearrange("(g p i) u -> g p i u", i=GROUP_BLOCKS, p=P)
    w_groups = w_gcn.rearrange("(g p i) c -> g p i c", i=GROUP_BLOCKS, p=P)

    with (
        tc.tile_pool(name="held", bufs=1) as held,
        tc.psum_pool(name="psum", bufs=2) as psum,
        tc.psum_pool(name="psum_z", bufs=2 * PAIR) as psum_z,
    ):
        identity = held.tile([P, P], F32, name="identity")
        make_identity(nc, identity[:])

        x_raw = [held.tile([P, GROUP_BLOCKS, U], F32, name=f"x_raw{g}") for g in range(GROUPS)]
        first_column = [FIRST_BLOCK[chunks[0]] * P for g, chunks in LOADS]
        width = [sum(CHUNK_BLOCKS[q] for q in chunks) * P for g, chunks in LOADS]
        w_raw = [held.tile([P, GROUP_BLOCKS, width[n]], F32, name=f"w_raw{n}") for n in range(len(LOADS))]
        windows = [held.tile([P, S], F32, name=f"window{b}") for b in range(BLOCKS)]
        offsets = held.tile([P, N // 16], U16, name="offsets")
        adj_rows = held.tile([P, NODE_BLOCKS, U], F32, name="adj_rows")

        def load_base(b):
            nc.sync.dma_start(windows[b][:], base_blocks[b // GROUP_BLOCKS][b % GROUP_BLOCKS])

        for n, (g, chunks) in enumerate(LOADS):
            if n < GROUPS:
                nc.sync.dma_start(x_raw[g][:], x_groups[g])
            nc.sync.dma_start(w_raw[n][:], w_groups[g][:, :, first_column[n] : first_column[n] + width[n]])
            if n == 0:
                nc.sync.dma_start(adj_rows[:], adj.rearrange("(t p) v -> p t v", p=P))
            if n == GROUPS - 1:
                nc.sync.dma_start(offsets[:], offs)
            if n >= FIRST_BASE_LOAD:
                load_base(n - FIRST_BASE_LOAD)
        for b in range(len(LOADS) - FIRST_BASE_LOAD, BLOCKS):
            load_base(b)

        eps = held.tile([P, 1], F32, name="eps")
        nc.vector.memset(eps[:], EPS)
        root_eps = held.tile([P, 1], F32, name="root_eps")
        nc.scalar.activation(root_eps[:], eps[:], ACT.Sqrt)
        deg = held.tile([P, NODE_BLOCKS], F32, name="deg")
        nc.vector.reduce_sum(deg[:], adj_rows[:], axis=mybir.AxisListType.X)
        root = held.tile([P, NODE_BLOCKS], F32, name="root")
        nc.scalar.activation(root[:], deg[:], ACT.Sqrt, bias=eps[:])
        d = held.tile([P, NODE_BLOCKS], F32, name="d")
        nc.vector.reciprocal(d[:], root[:])
        scaled_rows = held.tile([P, U], F32, name="scaled_rows")
        nc.vector.tensor_scalar_mul(scaled_rows[:], adj_rows[:, 0, :], d[:, 0:1])
        flipped = psum_z.tile([P, NODE_BLOCKS, N], F32, name="flipped", tag="z_acc")
        ahat_t = held.tile([P, NODE_BLOCKS, N], BF16, name="ahat_t")
        for t in range(NODE_BLOCKS):
            nc.tensor.transpose(flipped[:, t, :], scaled_rows[:, t * P : (t + 1) * P], identity[:])
            nc.vector.tensor_scalar_mul(ahat_t[:, t, :], flipped[:, t, :], d[:, t : t + 1])

        def cast_shared(name, raw, first_engine):
            width = raw.shape[2]
            by_first = held.tile([P, width], BF16, name=f"{name}_f")
            by_scalar = held.tile([P, width], BF16, name=f"{name}_s")
            first_engine.tensor_copy(by_first[:], raw[:, 0, :])
            nc.scalar.copy(by_scalar[:], raw[:, 1, :])
            return [by_first[:], by_scalar[:]]

        x_bf = {}
        w_bf = {}
        h_acc = {}
        half_relu = {}

        def cast(n):
            g, chunks = LOADS[n]
            if n < GROUPS:
                x_bf[g] = cast_shared(f"x_bf{g}", x_raw[g], nc.vector)
            blocks = cast_shared(f"w_bf{n}", w_raw[n], nc.vector if n <= FIRST_BASE_LOAD else nc.gpsimd)
            for q in chunks:
                first = FIRST_BLOCK[q] * P - first_column[n]
                w_bf[q, g] = [block[:, first : first + CHUNK_BLOCKS[q] * P] for block in blocks]

        def accumulate(s):
            q, g = STEPS[s]
            chunk_width = CHUNK_BLOCKS[q] * P
            first_group = s % GROUPS == 0
            last_group = s % GROUPS == GROUPS - 1
            if first_group:
                h_acc[q] = [psum.tile([P, WIDEST * P], F32, name=f"h_acc{t}") for t in range(NODE_BLOCKS)]
            for b in range(GROUP_BLOCKS):
                for t in range(NODE_BLOCKS):
                    nc.tensor.matmul(
                        h_acc[q][t][:, 0:chunk_width],
                        x_bf[g][b][:, t * P : (t + 1) * P],
                        w_bf[q, g][b],
                        start=(first_group and b == 0),
                        stop=(last_group and b == GROUP_BLOCKS - 1),
                    )

        def aggregate(q):
            for first in range(0, CHUNK_BLOCKS[q], PAIR):
                aggregate_pair(q, range(first, first + PAIR))

        def aggregate_pair(q, blocks):
            h_bf = {i: [held.tile([P, P], BF16, name=f"h_bf{q}_{i}_{t}") for t in range(NODE_BLOCKS)] for i in blocks}
            for i in blocks:
                first = (i // GROUP_BLOCKS) * GROUP_BLOCKS * P + i % GROUP_BLOCKS
                columns = slice(first, first + GROUP_BLOCKS * (P - 1) + 1, GROUP_BLOCKS)
                if q == 0:
                    nc.vector.tensor_copy(h_bf[i][0][:], h_acc[q][0][:, columns])
                else:
                    nc.scalar.copy(h_bf[i][0][:], h_acc[q][0][:, columns])
                nc.scalar.copy(h_bf[i][1][:], h_acc[q][1][:, columns])
            z_acc = {i: psum_z.tile([P, N], F32, name="z_acc") for i in blocks}
            for t in range(NODE_BLOCKS):
                for i in blocks:
                    nc.tensor.matmul(
                        z_acc[i][:],
                        h_bf[i][t][:],
                        ahat_t[:, t, :],
                        start=(t == 0),
                        stop=(t == NODE_BLOCKS - 1),
                    )
            for i in blocks:
                b = FIRST_BLOCK[q] + i
                half_relu[b] = held.tile([P, N], F32, name=f"half_relu{b}")
                nc.scalar.activation(half_relu[b][:], z_acc[i][:], ACT.Relu, scale=BETA)

        def place(q, i):
            b = FIRST_BLOCK[q] + i
            nc.vector.tensor_tensor(
                windows[b][:].indirect(offsets[:]),
                x_raw[b // GROUP_BLOCKS][:, b % GROUP_BLOCKS, 0:N],
                half_relu[b][:],
                mybir.AluOpType.add,
            )
            nc.sync.dma_start(out_blocks[b // GROUP_BLOCKS][b % GROUP_BLOCKS], windows[b][:])

        for n in range(CAST_AHEAD):
            cast(n)
        for s in range(len(STEPS) + 1 + CHUNK_BLOCKS[-1]):
            if s + CAST_AHEAD < len(LOADS):
                cast(s + CAST_AHEAD)
            if s < len(STEPS):
                accumulate(s)
            for q in range(CHUNKS):
                since_complete = s - (q + 1) * GROUPS
                if since_complete == 0:
                    aggregate(q)
                if 1 <= since_complete <= CHUNK_BLOCKS[q]:
                    place(q, since_complete - 1)
